import numpy as np
import ml_dtypes


def mxq(x, axis, fmt="e4m3"):
    dtype, down = {"e4m3": (ml_dtypes.float8_e4m3fn, 7), "e5m2": (ml_dtypes.float8_e5m2, 14)}[fmt]
    v = np.moveaxis(np.asarray(x, np.float32).astype(ml_dtypes.bfloat16).astype(np.float64), axis, -1)
    blocks = v.reshape(v.shape[:-1] + (-1, 32))
    amax = np.abs(blocks).max(-1, keepdims=True)
    byte = np.maximum(np.where(amax > 0, np.frexp(amax)[1] - 1 + 127, 0) - down, 1)
    scale = np.exp2(byte - 127.0)
    codes = (blocks / scale).astype(np.float32).astype(dtype).astype(np.float64)
    return np.moveaxis((codes * scale).reshape(v.shape), -1, axis)


WIDE = False


def mx_kscale(k):
    if not WIDE:
        return np.ones(k)
    levels = np.array([10, -10, 5, -5, 0])
    if k % 512:
        return np.exp2(np.random.permutation(np.resize(levels, k // 32))).repeat(32)
    a = np.empty((k // 512, 16))
    for p in range(k // 512):
        a[p, :8] = np.random.permutation(np.resize(levels, 8))
        for g in range(8):
            far = levels[np.abs(levels - a[p, g]) >= 10]
            a[p, g + 8] = far[np.random.randint(len(far))]
    return np.exp2(a.ravel()).repeat(32)


BF16 = ml_dtypes.bfloat16


def bf(x):
    return np.asarray(x, np.float32).astype(BF16)


def f64(x):
    return np.asarray(x).astype(np.float64)


SL, BS, DM, H, NH, DO = 32, 128, 1024, 16, 64, 1024
DP = H * NH


def log_softmax0(x):
    z = x - x.max(0, keepdims=True)
    return z - np.log(np.exp(z).sum(0, keepdims=True))


def setup_inputs():
    s, u = mx_kscale(DM), mx_kscale(DM)
    return {"query": bf(np.random.standard_normal((BS, DM)) * 2.0 * s),
            "keys": bf(np.random.standard_normal((SL, BS, DM)) * u),
            "Wq": bf(np.random.standard_normal((DP, DM)) / np.sqrt(DM) / s),
            "Wk": bf(np.random.standard_normal((DP, DM)) / np.sqrt(DM) / u)}


def reference(query, keys, Wq, Wk):
    qp = mxq(f64(query), 1, "e4m3") @ mxq(f64(Wq), 1, "e4m3").T
    kp = mxq(f64(keys), 2, "e4m3") @ mxq(f64(Wk), 1, "e4m3").T
    dot = (qp * kp).reshape(SL, BS, H, NH).sum(-1) / np.sqrt(NH)
    return log_softmax0(dot)

@@ -1,0 +1,206 @@
+from contextlib import ExitStack
+
+import concourse.mybir as mybir
+from concourse.masks import make_identity
+
+F32 = mybir.dt.float32
+BF16 = mybir.dt.bfloat16
+U32 = mybir.dt.uint32
+U8 = mybir.dt.uint8
+FP8X4 = mybir.dt.float8_e4m3fn_x4
+ALU = mybir.AluOpType
+ACT = mybir.ActivationFunctionType
+AXIS_X = mybir.AxisListType.X
+
+P = 128
+PACK = 4
+SEQ = 32
+FEAT = 1024
+HEADS = 16
+HEAD_DIM = 64
+CHAN = HEADS * HEAD_DIM
+PASSES = FEAT // (P * PACK)
+ROUND = 2
+ROUNDS = SEQ // ROUND
+GROUP = ROUND * P
+GROUPS = CHAN // GROUP
+BANK = 512
+HALVES = CHAN // BANK
+BANK_HEADS = BANK // HEAD_DIM
+BANK_GROUPS = BANK // GROUP
+FOLD_WIDTHS = (32, 16, 8)
+
+FLOPS = 2 * (SEQ + 1) * P * FEAT * CHAN
+
+
+def tile_multiheadattention_pa_kernel(tc, query, keys, Wq, Wk, out):
+    nc = tc.nc
+    with ExitStack() as ctx:
+        ctx.enter_context(tc.manual_schedule())
+        raw = ctx.enter_context(tc.tile_pool(name="raw", bufs=1))
+        keep = ctx.enter_context(tc.tile_pool(name="keep", bufs=1))
+        stages = ctx.enter_context(tc.tile_pool(name="stages", bufs=4))
+        packed = ctx.enter_context(tc.tile_pool(name="packed", bufs=3))
+        prods = ctx.enter_context(tc.tile_pool(name="prods", bufs=6))
+        folds = ctx.enter_context(tc.tile_pool(name="folds", bufs=3))
+        scrap = ctx.enter_context(tc.tile_pool(name="scrap", bufs=2))
+        psum = ctx.enter_context(tc.psum_pool(name="psum", bufs=1))
+
+        query_raw = raw.tile([P, 1, FEAT], BF16)
+        nc.sync.dma_start(out=query_raw[:, 0, :], in_=query)
+        weight_raw = {}
+        for name, weight in (("wq", Wq), ("wk", Wk)):
+            for c in range(GROUPS):
+                rows = raw.tile([P, ROUND, FEAT], BF16, name="%s_raw%d" % (name, c))
+                nc.sync.dma_start(
+                    out=rows,
+                    in_=weight[c * GROUP : (c + 1) * GROUP, :].rearrange("(i p) k -> p i k", p=P),
+                )
+                weight_raw[(name, c)] = rows
+        keys_raw = []
+        for r in range(ROUNDS):
+            rows = raw.tile([P, ROUND, FEAT], BF16, name="keys_raw%d" % r)
+            nc.sync.dma_start(
+                out=rows, in_=keys[r * ROUND : (r + 1) * ROUND].rearrange("s b k -> b s k")
+            )
+            keys_raw.append(rows)
+
+        ident = keep.tile([P, P], F32)
+        make_identity(nc, ident)
+
+        warm = keep.tile([P, 1], F32)
+        nc.vector.memset(warm, 0.0)
+        nc.scalar.activation(out=warm, in_=warm, func=ACT.Exp)
+
+        def transpose_and_regroup(rows, bank_tag, bank_bufs, vector_helps):
+            n = rows.shape[1]
+            stage = stages.tile([P, PASSES, n, P, PACK], BF16, align_bytes=64, tag="stage%d" % n)
+            stage_words = stage.bitcast(F32)
+            for i in range(n):
+                words = rows[:, i, :].bitcast(F32)
+                bank = psum.tile([P, PASSES, 2, P], F32, tag=bank_tag, bufs=bank_bufs)
+                for g in range(PASSES):
+                    for u in range(2):
+                        every_second = words[:, 2 * g * P + u : 2 * (g + 1) * P : 2]
+                        nc.tensor.transpose(bank[:, g, u, :], every_second, ident)
+                if vector_helps and i % 2 == 1:
+                    nc.vector.tensor_copy(
+                        out=stage_words[:, :, i, :, :], in_=bank.rearrange("p g u r -> p g r u")
+                    )
+                else:
+                    nc.scalar.copy(
+                        out=stage_words[:, :, i, :, :], in_=bank.rearrange("p g u r -> p g r u")
+                    )
+            return stage
+
+        def quantise(stage, pool, name):
+            n = stage.shape[2]
+            codes = pool.tile([P, PASSES, n, P], U32, align_bytes=64, name="%s_codes" % name)
+            scales = pool.tile([P, PASSES, n, P], U8, align_bytes=64, name="%s_scales" % name)
+            nc.vector.quantize_mx(
+                out=codes.rearrange("p g i r -> p (g i r)").bitcast(FP8X4),
+                scales=scales.rearrange("p g i r -> p (g i r)"),
+                in_=stage.rearrange("p g i r t -> p (g i r t)"),
+            )
+            return codes, scales
+
+        q_mx = quantise(transpose_and_regroup(query_raw, "kp", 6, False), keep, "q")
+        w_mx = {}
+        for name in ("wq", "wk"):
+            for c in range(GROUPS):
+                stage = transpose_and_regroup(weight_raw[(name, c)], "kp", 6, False)
+                w_mx[(name, c)] = quantise(stage, keep, "%s%d" % (name, c))
+
+        def project(bank, rows_mx, i, name, half):
+            codes, scales = rows_mx
+            for c in range(BANK_GROUPS):
+                w_codes, w_scales = w_mx[(name, half * BANK_GROUPS + c)]
+                for g in range(PASSES):
+                    nc.tensor.matmul_mx(
+                        out=bank[:, c * GROUP : (c + 1) * GROUP],
+                        lhsT=codes[:, g, i, :].bitcast(FP8X4),
+                        lhsT_scale=scales[:, g, i, :],
+                        rhs=w_codes[:, g].rearrange("p i r -> p (i r)").bitcast(FP8X4),
+                        rhs_scale=w_scales[:, g].rearrange("p i r -> p (i r)"),
+                        start=(g == 0),
+                        stop=(g == PASSES - 1),
+                    )
+
+        qp = keep.tile([P, HALVES, BANK_HEADS, HEAD_DIM], F32)
+        for half in range(HALVES):
+            qp_bank = psum.tile([P, BANK_HEADS, HEAD_DIM], F32, tag="kp", bufs=6)
+            project(qp_bank.rearrange("p h j -> p (h j)"), q_mx, 0, "wq", half)
+            if half % 2 == 1:
+                nc.vector.tensor_scalar_mul(out=qp[:, half], in0=qp_bank, scalar1=HEAD_DIM**-0.5)
+            else:
+                nc.scalar.activation(out=qp[:, half], in_=qp_bank, func=ACT.Copy, scale=HEAD_DIM**-0.5)
+
+        dot = keep.tile([P, SEQ, HEADS], F32)
+        key_stage = {}
+        key_mx = {}
+        products = {}
+        for r in range(-2, ROUNDS + 1):
+            if 0 <= r + 1 < ROUNDS:
+                key_mx[r + 1] = quantise(key_stage[r + 1], packed, "key")
+            if 0 <= r < ROUNDS:
+                for i in range(ROUND):
+                    product = prods.tile([P, HALVES, BANK_HEADS, HEAD_DIM], F32)
+                    for half in range(HALVES):
+                        kp = psum.tile([P, BANK_HEADS, HEAD_DIM], F32, tag="kp", bufs=6)
+                        project(kp.rearrange("p h j -> p (h j)"), key_mx[r], i, "wk", half)
+                        nc.vector.tensor_tensor(out=product[:, half], in0=kp, in1=qp[:, half], op=ALU.mult)
+                    products[(r, i)] = product.rearrange("p n h j -> p (n h) j")
+            if 0 <= r - 1:
+                for i in range(ROUND):
+                    s = (r - 1) * ROUND + i
+                    product = products[(r - 1, i)]
+                    if i % 2 == 0:
+                        for width in FOLD_WIDTHS:
+                            folded = folds.tile([P, HEADS, width], F32, tag="folded%d" % width)
+                            nc.gpsimd.tensor_tensor(
+                                out=folded,
+                                in0=product[:, :, 0:width],
+                                in1=product[:, :, width : 2 * width],
+                                op=ALU.add,
+                            )
+                            product = folded
+                        nc.vector.tensor_reduce(out=dot[:, s, :], in_=product, axis=AXIS_X, op=ALU.add)
+                    else:
+                        unread = scrap.tile([P, HEADS, HEAD_DIM], F32)
+                        for h in range(HEADS):
+                            nc.scalar.activation(
+                                out=unread[:, h, :],
+                                in_=product[:, h, :],
+                                func=ACT.Copy,
+                                accum_out=dot[:, s, h : h + 1],
+                            )
+            if r + 2 < ROUNDS:
+                key_stage[r + 2] = transpose_and_regroup(keys_raw[r + 2], "xt", 2, r < 0)
+
+        by_head = "p s h -> p h s"
+        top = keep.tile([P, HEADS], F32)
+        nc.vector.tensor_reduce(out=top, in_=dot.rearrange(by_head), axis=AXIS_X, op=ALU.max)
+        shifted = keep.tile([P, SEQ, HEADS], F32)
+        nc.vector.tensor_tensor(
+            out=shifted, in0=dot, in1=top.unsqueeze(1).to_broadcast([P, SEQ, HEADS]), op=ALU.subtract
+        )
+        grown = keep.tile([P, SEQ, HEADS], F32)
+        nc.scalar.activation(out=grown, in_=shifted, func=ACT.Exp)
+        nc.scalar.activation(out=warm, in_=warm, func=ACT.Ln)
+        total = keep.tile([P, HEADS], F32)
+        nc.vector.tensor_reduce(out=total, in_=grown.rearrange(by_head), axis=AXIS_X, op=ALU.add)
+        log_total = keep.tile([P, HEADS], F32)
+        nc.scalar.activation(out=log_total, in_=total, func=ACT.Ln)
+        result = keep.tile([P, SEQ, HEADS], F32)
+        part = SEQ // 2
+        for first, queue in ((0, nc.sync), (part, nc.scalar)):
+            nc.vector.tensor_tensor(
+                out=result[:, first : first + part, :],
+                in0=shifted[:, first : first + part, :],
+                in1=log_total.unsqueeze(1).to_broadcast([P, part, HEADS]),
+                op=ALU.subtract,
+            )
+            queue.dma_start(
+                out=out[first : first + part].rearrange("s b h -> b s h"),
+                in_=result[:, first : first + part, :],
+            )

@@ -20,14 +20,11 @@ HEADS = 16
 HEAD_DIM = 64
 CHAN = HEADS * HEAD_DIM
 PASSES = FEAT // (P * PACK)
-ROUND = 2
-ROUNDS = SEQ // ROUND
-GROUP = ROUND * P
-GROUPS = CHAN // GROUP
-BANK = 512
-HALVES = CHAN // BANK
+PAIR = 2
+QUAD = 4
+HALVES = 2
+BANK = CHAN // HALVES
 BANK_HEADS = BANK // HEAD_DIM
-BANK_GROUPS = BANK // GROUP
 FOLD_WIDTHS = (32, 16, 8)
 
 FLOPS = 2 * (SEQ + 1) * P * FEAT * CHAN
@@ -39,31 +36,30 @@ def tile_multiheadattention_pa_kernel(tc, query, keys, Wq, Wk, out):
         ctx.enter_context(tc.manual_schedule())
         raw = ctx.enter_context(tc.tile_pool(name="raw", bufs=1))
         keep = ctx.enter_context(tc.tile_pool(name="keep", bufs=1))
-        stages = ctx.enter_context(tc.tile_pool(name="stages", bufs=4))
-        packed = ctx.enter_context(tc.tile_pool(name="packed", bufs=3))
-        prods = ctx.enter_context(tc.tile_pool(name="prods", bufs=6))
-        folds = ctx.enter_context(tc.tile_pool(name="folds", bufs=3))
+        stages = ctx.enter_context(tc.tile_pool(name="stages", bufs=6))
+        packed = ctx.enter_context(tc.tile_pool(name="packed", bufs=4))
+        prods = ctx.enter_context(tc.tile_pool(name="prods", bufs=7))
+        folds = ctx.enter_context(tc.tile_pool(name="folds", bufs=2))
         scrap = ctx.enter_context(tc.tile_pool(name="scrap", bufs=2))
-        psum = ctx.enter_context(tc.psum_pool(name="psum", bufs=1))
+        psum = ctx.enter_context(tc.psum_pool(name="psum", bufs=4))
 
-        query_raw = raw.tile([P, 1, FEAT], BF16)
-        nc.sync.dma_start(out=query_raw[:, 0, :], in_=query)
-        weight_raw = {}
+        raw_tiles = {}
+
+        def load_pair(name, first, source):
+            rows = raw.tile([P, PAIR, FEAT], BF16, name="%s_raw%d" % (name, first))
+            nc.sync.dma_start(out=rows, in_=source)
+            for i in range(PAIR):
+                raw_tiles[(name, first + i)] = rows[:, i, :]
+
+        query_raw = raw.tile([P, FEAT], BF16)
+        nc.sync.dma_start(out=query_raw, in_=query)
+        raw_tiles[("q", 0)] = query_raw
         for name, weight in (("wq", Wq), ("wk", Wk)):
-            for c in range(GROUPS):
-                rows = raw.tile([P, ROUND, FEAT], BF16, name="%s_raw%d" % (name, c))
-                nc.sync.dma_start(
-                    out=rows,
-                    in_=weight[c * GROUP : (c + 1) * GROUP, :].rearrange("(i p) k -> p i k", p=P),
-                )
-                weight_raw[(name, c)] = rows
-        keys_raw = []
-        for r in range(ROUNDS):
-            rows = raw.tile([P, ROUND, FEAT], BF16, name="keys_raw%d" % r)
-            nc.sync.dma_start(
-                out=rows, in_=keys[r * ROUND : (r + 1) * ROUND].rearrange("s b k -> b s k")
-            )
-            keys_raw.append(rows)
+            for first in range(0, CHAN // P, PAIR):
+                source = weight[first * P : (first + PAIR) * P, :]
+                load_pair(name, first, source.rearrange("(i p) k -> p i k", p=P))
+        for s in range(0, SEQ, PAIR):
+            load_pair("k", s, keys[s : s + PAIR].rearrange("s b k -> b s k"))
 
         ident = keep.tile([P, P], F32)
         make_identity(nc, ident)
@@ -72,123 +68,188 @@ def tile_multiheadattention_pa_kernel(tc, query, keys, Wq, Wk, out):
         nc.vector.memset(warm, 0.0)
         nc.scalar.activation(out=warm, in_=warm, func=ACT.Exp)
 
-        def transpose_and_regroup(rows, bank_tag, bank_bufs, vector_helps):
-            n = rows.shape[1]
-            stage = stages.tile([P, PASSES, n, P, PACK], BF16, align_bytes=64, tag="stage%d" % n)
-            stage_words = stage.bitcast(F32)
-            for i in range(n):
-                words = rows[:, i, :].bitcast(F32)
-                bank = psum.tile([P, PASSES, 2, P], F32, tag=bank_tag, bufs=bank_bufs)
-                for g in range(PASSES):
-                    for u in range(2):
-                        every_second = words[:, 2 * g * P + u : 2 * (g + 1) * P : 2]
-                        nc.tensor.transpose(bank[:, g, u, :], every_second, ident)
-                if vector_helps and i % 2 == 1:
-                    nc.vector.tensor_copy(
-                        out=stage_words[:, :, i, :, :], in_=bank.rearrange("p g u r -> p g r u")
-                    )
-                else:
-                    nc.scalar.copy(
-                        out=stage_words[:, :, i, :, :], in_=bank.rearrange("p g u r -> p g r u")
-                    )
-            return stage
+        def transpose_tile(name, i, tag):
+            words = raw_tiles[(name, i)].bitcast(F32)
+            bank = psum.tile([P, PASSES, 2, P], F32, tag=tag)
+            for g in range(PASSES):
+                for u in range(2):
+                    every_second = words[:, 2 * g * P + u : 2 * (g + 1) * P : 2]
+                    nc.tensor.transpose(bank[:, g, u, :], every_second, ident)
+            return bank
 
-        def quantise(stage, pool, name):
-            n = stage.shape[2]
-            codes = pool.tile([P, PASSES, n, P], U32, align_bytes=64, name="%s_codes" % name)
-            scales = pool.tile([P, PASSES, n, P], U8, align_bytes=64, name="%s_scales" % name)
+        def empty_bank(bank, stage, i, on_vector):
+            target = stage.bitcast(F32)[:, :, i, :, :]
+            if on_vector:
+                nc.vector.tensor_copy(out=target, in_=bank.rearrange("p g u r -> p g r u"))
+            else:
+                nc.scalar.copy(out=target, in_=bank.rearrange("p g u r -> p g r u"))
+
+        def quantise(stage_part, codes_part, scales_part):
             nc.vector.quantize_mx(
-                out=codes.rearrange("p g i r -> p (g i r)").bitcast(FP8X4),
-                scales=scales.rearrange("p g i r -> p (g i r)"),
-                in_=stage.rearrange("p g i r t -> p (g i r t)"),
+                out=codes_part.bitcast(FP8X4), scales=scales_part, in_=stage_part
             )
-            return codes, scales
 
-        q_mx = quantise(transpose_and_regroup(query_raw, "kp", 6, False), keep, "q")
-        w_mx = {}
+        operand = {}
+
+        def quantise_rows(stage, name, first, pool):
+            count = stage.shape[2]
+            codes = pool.tile([P, PASSES, count * P], U32, align_bytes=64, name="%s_codes" % name)
+            scales = pool.tile([P, PASSES, count * P], U8, align_bytes=64, name="%s_scales" % name)
+            quantise(
+                stage.rearrange("p g i r t -> p (g i r t)"),
+                codes.rearrange("p g c -> p (g c)"),
+                scales.rearrange("p g c -> p (g c)"),
+            )
+            for i in range(count):
+                cols = slice(i * P, (i + 1) * P)
+                operand[(name, first + i)] = (codes[:, :, cols], scales[:, :, cols])
+
+        weight_mx = {}
         for name in ("wq", "wk"):
-            for c in range(GROUPS):
-                stage = transpose_and_regroup(weight_raw[(name, c)], "kp", 6, False)
-                w_mx[(name, c)] = quantise(stage, keep, "%s%d" % (name, c))
+            for half in range(HALVES):
+                weight_mx[(name, half)] = (
+                    keep.tile([P, PASSES, BANK], U32, align_bytes=64, name="%s_codes%d" % (name, half)),
+                    keep.tile([P, PASSES, BANK], U8, align_bytes=64, name="%s_scales%d" % (name, half)),
+                )
 
-        def project(bank, rows_mx, i, name, half):
-            codes, scales = rows_mx
-            for c in range(BANK_GROUPS):
-                w_codes, w_scales = w_mx[(name, half * BANK_GROUPS + c)]
-                for g in range(PASSES):
-                    nc.tensor.matmul_mx(
-                        out=bank[:, c * GROUP : (c + 1) * GROUP],
-                        lhsT=codes[:, g, i, :].bitcast(FP8X4),
-                        lhsT_scale=scales[:, g, i, :],
-                        rhs=w_codes[:, g].rearrange("p i r -> p (i r)").bitcast(FP8X4),
-                        rhs_scale=w_scales[:, g].rearrange("p i r -> p (i r)"),
-                        start=(g == 0),
-                        stop=(g == PASSES - 1),
-                    )
+        def quantise_weight_pair(stage, name, first):
+            codes, scales = weight_mx[(name, first // QUAD)]
+            cols = slice(first % QUAD * P, (first % QUAD + PAIR) * P)
+            for g in range(PASSES):
+                quantise(stage[:, g].rearrange("p i r t -> p (i r t)"), codes[:, g, cols], scales[:, g, cols])
+
+        def transpose_run(name, first, count, tags, vector_helps):
+            banks = [transpose_tile(name, first + i, tags[i % len(tags)]) for i in range(count)]
+            result = []
+            for pair in range(count // PAIR):
+                stage = stages.tile([P, PASSES, PAIR, P, PACK], BF16, align_bytes=64)
+                for i in range(PAIR):
+                    empty_bank(banks[pair * PAIR + i], stage, i, vector_helps and i % 2 == 1)
+                result.append(stage)
+            return result
+
+        def project(rows, weight_name, half, tag):
+            codes, scales = operand[rows]
+            w_codes, w_scales = weight_mx[(weight_name, half)]
+            bank = psum.tile([P, BANK], F32, tag=tag)
+            for g in range(PASSES):
+                nc.tensor.matmul_mx(
+                    out=bank,
+                    lhsT=codes[:, g, :].bitcast(FP8X4),
+                    lhsT_scale=scales[:, g, :],
+                    rhs=w_codes[:, g, :].bitcast(FP8X4),
+                    rhs_scale=w_scales[:, g, :],
+                    start=(g == 0),
+                    stop=(g == PASSES - 1),
+                )
+            return bank.rearrange("p (h j) -> p h j", j=HEAD_DIM)
+
+        query_stage = stages.tile([P, PASSES, 1, P, PACK], BF16, align_bytes=64, tag="query_stage", bufs=1)
+        empty_bank(transpose_tile("q", 0, "xt"), query_stage, 0, False)
+        previous = None
+        for name in ("wq", "wk"):
+            for first in range(0, CHAN // P, PAIR):
+                stage = transpose_run(name, first, PAIR, ("kp", "xt"), first % QUAD == 0)[0]
+                if previous is None:
+                    quantise_rows(query_stage, "q", 0, keep)
+                else:
+                    quantise_weight_pair(*previous)
+                previous = (stage, name, first)
 
         qp = keep.tile([P, HALVES, BANK_HEADS, HEAD_DIM], F32)
+        dot = keep.tile([P, HEADS, SEQ], F32)
+
+        def multiply(s):
+            product = prods.tile([P, HALVES, BANK_HEADS, HEAD_DIM], F32)
+            for half in range(HALVES):
+                kp = project(("k", s), "wk", half, "kp")
+                nc.vector.tensor_tensor(out=product[:, half], in0=kp, in1=qp[:, half], op=ALU.mult)
+            return product.rearrange("p n h j -> p (n h) j")
+
+        def sum_on_scalar(product, s):
+            unread = scrap.tile([P, HEADS, HEAD_DIM], F32)
+            for h in range(HEADS):
+                nc.scalar.activation(
+                    out=unread[:, h, :], in_=product[:, h, :], func=ACT.Copy, accum_out=dot[:, h, s : s + 1]
+                )
+
+        def sum_on_vector(product, s):
+            nc.vector.tensor_reduce(out=dot[:, :, s], in_=product, axis=AXIS_X, op=ALU.add)
+
+        def fold_on_gpsimd(product):
+            for width in FOLD_WIDTHS:
+                folded = folds.tile([P, HEADS, width], F32, tag="folded%d" % width)
+                nc.gpsimd.tensor_tensor(
+                    out=folded, in0=product[:, :, 0:width], in1=product[:, :, width : 2 * width], op=ALU.add
+                )
+                product = folded
+            return product
+
+        chunks = [(s, 2) for s in range(0, SEQ, 2)]
+        summers = "GS" * 14 + "SGSV"
+        to_sum = []
+        folded_tiles = []
+        staged = {}
+
+        def transpose_chunk(n):
+            if n < len(chunks):
+                first, count = chunks[n]
+                new_stages = transpose_run("k", first, count, ("xt",), False)
+                for pair, stage in enumerate(new_stages):
+                    staged[first + pair * PAIR] = stage
+
+        transpose_chunk(0)
+        quantise_weight_pair(*previous)
         for half in range(HALVES):
-            qp_bank = psum.tile([P, BANK_HEADS, HEAD_DIM], F32, tag="kp", bufs=6)
-            project(qp_bank.rearrange("p h j -> p (h j)"), q_mx, 0, "wq", half)
-            if half % 2 == 1:
-                nc.vector.tensor_scalar_mul(out=qp[:, half], in0=qp_bank, scalar1=HEAD_DIM**-0.5)
-            else:
-                nc.scalar.activation(out=qp[:, half], in_=qp_bank, func=ACT.Copy, scale=HEAD_DIM**-0.5)
+            bank = project(("q", 0), "wq", half, "kp")
+            nc.scalar.activation(out=qp[:, half], in_=bank, func=ACT.Copy, scale=HEAD_DIM**-0.5)
+        quantise_rows(staged[0], "k", 0, packed)
+        transpose_chunk(1)
+        for n in range(len(chunks)):
+            if n > 0:
+                transpose_chunk(n + 2 - 0)
+            waiting = []
+            if n + 1 < len(chunks):
+                waiting = [chunks[n + 1][0] + i for i in range(0, chunks[n + 1][1], PAIR)]
+            fresh = []
+            for i in range(chunks[n][1]):
+                s = chunks[n][0] + i
+                if n > 0 and i % PAIR == 0 and waiting:
+                    quantise_rows(staged[waiting[0]], "k", waiting.pop(0), packed)
+                product = multiply(s)
+                if summers[s] == "G":
+                    folded_tiles.append((fold_on_gpsimd(product), s))
+                elif summers[s] == "V":
+                    sum_on_vector(product, s)
+                else:
+                    fresh.append((product, s))
+                if i % 2 == 1 and len(folded_tiles) > 1:
+                    sum_on_vector(*folded_tiles.pop(0))
+            while waiting:
+                quantise_rows(staged[waiting[0]], "k", waiting.pop(0), packed)
+            if n == 0:
+                transpose_chunk(2)
+            for product, s in fresh:
+                sum_on_scalar(product, s)
+        while folded_tiles:
+            sum_on_vector(*folded_tiles.pop(0))
 
-        dot = keep.tile([P, SEQ, HEADS], F32)
-        key_stage = {}
-        key_mx = {}
-        products = {}
-        for r in range(-2, ROUNDS + 1):
-            if 0 <= r + 1 < ROUNDS:
-                key_mx[r + 1] = quantise(key_stage[r + 1], packed, "key")
-            if 0 <= r < ROUNDS:
-                for i in range(ROUND):
-                    product = prods.tile([P, HALVES, BANK_HEADS, HEAD_DIM], F32)
-                    for half in range(HALVES):
-                        kp = psum.tile([P, BANK_HEADS, HEAD_DIM], F32, tag="kp", bufs=6)
-                        project(kp.rearrange("p h j -> p (h j)"), key_mx[r], i, "wk", half)
-                        nc.vector.tensor_tensor(out=product[:, half], in0=kp, in1=qp[:, half], op=ALU.mult)
-                    products[(r, i)] = product.rearrange("p n h j -> p (n h) j")
-            if 0 <= r - 1:
-                for i in range(ROUND):
-                    s = (r - 1) * ROUND + i
-                    product = products[(r - 1, i)]
-                    if i % 2 == 0:
-                        for width in FOLD_WIDTHS:
-                            folded = folds.tile([P, HEADS, width], F32, tag="folded%d" % width)
-                            nc.gpsimd.tensor_tensor(
-                                out=folded,
-                                in0=product[:, :, 0:width],
-                                in1=product[:, :, width : 2 * width],
-                                op=ALU.add,
-                            )
-                            product = folded
-                        nc.vector.tensor_reduce(out=dot[:, s, :], in_=product, axis=AXIS_X, op=ALU.add)
-                    else:
-                        unread = scrap.tile([P, HEADS, HEAD_DIM], F32)
-                        for h in range(HEADS):
-                            nc.scalar.activation(
-                                out=unread[:, h, :],
-                                in_=product[:, h, :],
-                                func=ACT.Copy,
-                                accum_out=dot[:, s, h : h + 1],
-                            )
-            if r + 2 < ROUNDS:
-                key_stage[r + 2] = transpose_and_regroup(keys_raw[r + 2], "xt", 2, r < 0)
-
-        by_head = "p s h -> p h s"
         top = keep.tile([P, HEADS], F32)
-        nc.vector.tensor_reduce(out=top, in_=dot.rearrange(by_head), axis=AXIS_X, op=ALU.max)
-        shifted = keep.tile([P, SEQ, HEADS], F32)
-        nc.vector.tensor_tensor(
-            out=shifted, in0=dot, in1=top.unsqueeze(1).to_broadcast([P, SEQ, HEADS]), op=ALU.subtract
-        )
-        grown = keep.tile([P, SEQ, HEADS], F32)
-        nc.scalar.activation(out=grown, in_=shifted, func=ACT.Exp)
-        nc.scalar.activation(out=warm, in_=warm, func=ACT.Ln)
+        shifted = keep.tile([P, HEADS, SEQ], F32)
+        grown = keep.tile([P, HEADS, SEQ], F32)
         total = keep.tile([P, HEADS], F32)
-        nc.vector.tensor_reduce(out=total, in_=grown.rearrange(by_head), axis=AXIS_X, op=ALU.add)
+        for half in range(HALVES):
+            heads = slice(half * BANK_HEADS, (half + 1) * BANK_HEADS)
+            nc.vector.tensor_reduce(out=top[:, heads], in_=dot[:, heads], axis=AXIS_X, op=ALU.max)
+            nc.vector.tensor_tensor(
+                out=shifted[:, heads],
+                in0=dot[:, heads],
+                in1=top[:, heads].unsqueeze(2).to_broadcast([P, BANK_HEADS, SEQ]),
+                op=ALU.subtract,
+            )
+            nc.scalar.activation(out=grown[:, heads], in_=shifted[:, heads], func=ACT.Exp)
+        nc.scalar.activation(out=warm, in_=warm, func=ACT.Ln)
+        nc.vector.tensor_reduce(out=total, in_=grown, axis=AXIS_X, op=ALU.add)
         log_total = keep.tile([P, HEADS], F32)
         nc.scalar.activation(out=log_total, in_=total, func=ACT.Ln)
         result = keep.tile([P, SEQ, HEADS], F32)
@@ -196,7 +257,7 @@ def tile_multiheadattention_pa_kernel(tc, query, keys, Wq, Wk, out):
         for first, queue in ((0, nc.sync), (part, nc.scalar)):
             nc.vector.tensor_tensor(
                 out=result[:, first : first + part, :],
-                in0=shifted[:, first : first + part, :],
+                in0=shifted[:, :, first : first + part].rearrange("p h s -> p s h"),
                 in1=log_total.unsqueeze(1).to_broadcast([P, part, HEADS]),
                 op=ALU.subtract,
             )

@@ -146,6 +146,13 @@ def tile_multiheadattention_pa_kernel(tc, query, keys, Wq, Wk, out):
 
         query_stage = stages.tile([P, PASSES, 1, P, PACK], BF16, align_bytes=64, tag="query_stage", bufs=1)
         empty_bank(transpose_tile("q", 0, "xt"), query_stage, 0, False)
+        qp = keep.tile([P, HALVES, BANK_HEADS, HEAD_DIM], F32)
+
+        def project_query():
+            for half in range(HALVES):
+                bank = project(("q", 0), "wq", half, "kp")
+                nc.scalar.activation(out=qp[:, half], in_=bank, func=ACT.Copy, scale=HEAD_DIM**-0.5)
+
         previous = None
         for name in ("wq", "wk"):
             for first in range(0, CHAN // P, PAIR):
@@ -155,16 +162,23 @@ def tile_multiheadattention_pa_kernel(tc, query, keys, Wq, Wk, out):
                 else:
                     quantise_weight_pair(*previous)
                 previous = (stage, name, first)
+                if (name, first) == ("wk", 99):
+                    project_query()
 
-        qp = keep.tile([P, HALVES, BANK_HEADS, HEAD_DIM], F32)
         dot = keep.tile([P, HEADS, SEQ], F32)
 
-        def multiply(s):
-            product = prods.tile([P, HALVES, BANK_HEADS, HEAD_DIM], F32)
-            for half in range(HALVES):
+        def multiply(tiles, by_half):
+            result = {}
+            for s in tiles:
+                product = prods.tile([P, HALVES, BANK_HEADS, HEAD_DIM], F32)
+                result[s] = product
+            order = [(s, half) for s in tiles for half in range(HALVES)]
+            if by_half:
+                order = [(s, half) for half in range(HALVES) for s in tiles]
+            for s, half in order:
                 kp = project(("k", s), "wk", half, "kp")
-                nc.vector.tensor_tensor(out=product[:, half], in0=kp, in1=qp[:, half], op=ALU.mult)
-            return product.rearrange("p n h j -> p (n h) j")
+                nc.vector.tensor_tensor(out=result[s][:, half], in0=kp, in1=qp[:, half], op=ALU.mult)
+            return {s: product.rearrange("p n h j -> p (n h) j") for s, product in result.items()}
 
         def sum_on_scalar(product, s):
             unread = scrap.tile([P, HEADS, HEAD_DIM], F32)
@@ -178,7 +192,7 @@ def tile_multiheadattention_pa_kernel(tc, query, keys, Wq, Wk, out):
 
         def fold_on_gpsimd(product):
             for width in FOLD_WIDTHS:
-                folded = folds.tile([P, HEADS, width], F32, tag="folded%d" % width)
+                folded = folds.tile([P, HEADS, width], F32, tag="folded%d" % width, bufs=4 if width == FOLD_WIDTHS[-1] else 2)
                 nc.gpsimd.tensor_tensor(
                     out=folded, in0=product[:, :, 0:width], in1=product[:, :, width : 2 * width], op=ALU.add
                 )
@@ -186,7 +200,7 @@ def tile_multiheadattention_pa_kernel(tc, query, keys, Wq, Wk, out):
             return product
 
         chunks = [(s, 2) for s in range(0, SEQ, 2)]
-        summers = "GS" * 14 + "SGSV"
+        summers = "SG" * 15 + "SV"
         to_sum = []
         folded_tiles = []
         staged = {}
@@ -200,11 +214,9 @@ def tile_multiheadattention_pa_kernel(tc, query, keys, Wq, Wk, out):
 
         transpose_chunk(0)
         quantise_weight_pair(*previous)
-        for half in range(HALVES):
-            bank = project(("q", 0), "wq", half, "kp")
-            nc.scalar.activation(out=qp[:, half], in_=bank, func=ACT.Copy, scale=HEAD_DIM**-0.5)
         quantise_rows(staged[0], "k", 0, packed)
         transpose_chunk(1)
+        project_query()
         for n in range(len(chunks)):
             if n > 0:
                 transpose_chunk(n + 2 - 0)
@@ -216,14 +228,18 @@ def tile_multiheadattention_pa_kernel(tc, query, keys, Wq, Wk, out):
                 s = chunks[n][0] + i
                 if n > 0 and i % PAIR == 0 and waiting:
                     quantise_rows(staged[waiting[0]], "k", waiting.pop(0), packed)
-                product = multiply(s)
+                if n == 0 and i == 0:
+                    product_of = multiply(list(range(chunks[0][1])), False)
+                elif n > 0:
+                    product_of = multiply([s], False)
+                product = product_of[s]
                 if summers[s] == "G":
                     folded_tiles.append((fold_on_gpsimd(product), s))
                 elif summers[s] == "V":
                     sum_on_vector(product, s)
                 else:
                     fresh.append((product, s))
-                if i % 2 == 1 and len(folded_tiles) > 1:
+                if i % 2 == 0 and len(folded_tiles) > 1:
                     sum_on_vector(*folded_tiles.pop(0))
             while waiting:
                 quantise_rows(staged[waiting[0]], "k", waiting.pop(0), packed)

@@ -190,14 +190,24 @@ def tile_multiheadattention_pa_kernel(tc, query, keys, Wq, Wk, out):
         def sum_on_vector(product, s):
             nc.vector.tensor_reduce(out=dot[:, :, s], in_=product, axis=AXIS_X, op=ALU.add)
 
-        def fold_on_gpsimd(product):
-            for width in FOLD_WIDTHS:
-                folded = folds.tile([P, HEADS, width], F32, tag="folded%d" % width, bufs=4 if width == FOLD_WIDTHS[-1] else 2)
-                nc.gpsimd.tensor_tensor(
-                    out=folded, in0=product[:, :, 0:width], in1=product[:, :, width : 2 * width], op=ALU.add
-                )
-                product = folded
-            return product
+        half_folded = []
+
+        def fold(source, width):
+            folded = folds.tile([P, HEADS, width], F32, tag="folded%d" % width, bufs=4 if width == FOLD_WIDTHS[-1] else 2)
+            nc.gpsimd.tensor_tensor(
+                out=folded, in0=source[:, :, 0:width], in1=source[:, :, width : 2 * width], op=ALU.add
+            )
+            return folded
+
+        def last_fold():
+            source, s = half_folded.pop()
+            folded_tiles.append((fold(source, FOLD_WIDTHS[2]), s))
+
+        def fold_on_gpsimd(product, s):
+            folded = fold(product, FOLD_WIDTHS[0])
+            if half_folded:
+                last_fold()
+            half_folded.append((fold(folded, FOLD_WIDTHS[1]), s))
 
         chunks = [(s, 2) for s in range(0, SEQ, 2)]
         summers = "SG" * 15 + "SV"
@@ -234,7 +244,9 @@ def tile_multiheadattention_pa_kernel(tc, query, keys, Wq, Wk, out):
                     product_of = multiply([s], False)
                 product = product_of[s]
                 if summers[s] == "G":
-                    folded_tiles.append((fold_on_gpsimd(product), s))
+                    fold_on_gpsimd(product, s)
+                    if s == 29:
+                        last_fold()
                 elif summers[s] == "V":
                     sum_on_vector(product, s)
                 else:

@@ -11,6 +11,7 @@ FP8X4 = mybir.dt.float8_e4m3fn_x4
 ALU = mybir.AluOpType
 ACT = mybir.ActivationFunctionType
 AXIS_X = mybir.AxisListType.X
+AXIS_XY = mybir.AxisListType.XY
 
 P = 128
 PACK = 4
@@ -21,11 +22,14 @@ HEAD_DIM = 64
 CHAN = HEADS * HEAD_DIM
 PASSES = FEAT // (P * PACK)
 PAIR = 2
-QUAD = 4
+PAIRS = SEQ // PAIR
+GROUP = PAIR * P
 HALVES = 2
 BANK = CHAN // HALVES
-BANK_HEADS = BANK // HEAD_DIM
-FOLD_WIDTHS = (32, 16, 8)
+BANK_PAIRS = BANK // GROUP
+GROUP_HEADS = GROUP // HEAD_DIM
+HALF_HEADS = HEADS // HALVES
+PART = HEAD_DIM // PAIR
 
 FLOPS = 2 * (SEQ + 1) * P * FEAT * CHAN
 
@@ -37,7 +41,7 @@ def tile_multiheadattention_pa_kernel(tc, query, keys, Wq, Wk, out):
         raw = ctx.enter_context(tc.tile_pool(name="raw", bufs=1))
         keep = ctx.enter_context(tc.tile_pool(name="keep", bufs=1))
         stages = ctx.enter_context(tc.tile_pool(name="stages", bufs=6))
-        packed = ctx.enter_context(tc.tile_pool(name="packed", bufs=4))
+        packed = ctx.enter_context(tc.tile_pool(name="packed", bufs=3))
         prods = ctx.enter_context(tc.tile_pool(name="prods", bufs=7))
         folds = ctx.enter_context(tc.tile_pool(name="folds", bufs=2))
         scrap = ctx.enter_context(tc.tile_pool(name="scrap", bufs=2))
@@ -57,7 +61,7 @@ def tile_multiheadattention_pa_kernel(tc, query, keys, Wq, Wk, out):
         for name, weight in (("wq", Wq), ("wk", Wk)):
             for first in range(0, CHAN // P, PAIR):
                 source = weight[first * P : (first + PAIR) * P, :]
-                load_pair(name, first, source.rearrange("(i p) k -> p i k", p=P))
+                load_pair(name, first, source.rearrange("(p i) k -> p i k", i=PAIR))
         for s in range(0, SEQ, PAIR):
             load_pair("k", s, keys[s : s + PAIR].rearrange("s b k -> b s k"))
 
@@ -84,10 +88,15 @@ def tile_multiheadattention_pa_kernel(tc, query, keys, Wq, Wk, out):
             else:
                 nc.scalar.copy(out=target, in_=bank.rearrange("p g u r -> p g r u"))
 
+        def transpose_pair(name, first, tags, vector_helps):
+            banks = [transpose_tile(name, first + i, tags[i]) for i in range(PAIR)]
+            stage = stages.tile([P, PASSES, PAIR, P, PACK], BF16, align_bytes=64)
+            for i in range(PAIR):
+                empty_bank(banks[i], stage, i, vector_helps and i == 1)
+            return stage
+
         def quantise(stage_part, codes_part, scales_part):
-            nc.vector.quantize_mx(
-                out=codes_part.bitcast(FP8X4), scales=scales_part, in_=stage_part
-            )
+            nc.vector.quantize_mx(out=codes_part.bitcast(FP8X4), scales=scales_part, in_=stage_part)
 
         operand = {}
 
@@ -113,25 +122,16 @@ def tile_multiheadattention_pa_kernel(tc, query, keys, Wq, Wk, out):
                 )
 
         def quantise_weight_pair(stage, name, first):
-            codes, scales = weight_mx[(name, first // QUAD)]
-            cols = slice(first % QUAD * P, (first % QUAD + PAIR) * P)
+            half, place = divmod(first // PAIR, BANK_PAIRS)
+            codes, scales = weight_mx[(name, half)]
+            cols = slice(place * GROUP, (place + 1) * GROUP)
             for g in range(PASSES):
                 quantise(stage[:, g].rearrange("p i r t -> p (i r t)"), codes[:, g, cols], scales[:, g, cols])
 
-        def transpose_run(name, first, count, tags, vector_helps):
-            banks = [transpose_tile(name, first + i, tags[i % len(tags)]) for i in range(count)]
-            result = []
-            for pair in range(count // PAIR):
-                stage = stages.tile([P, PASSES, PAIR, P, PACK], BF16, align_bytes=64)
-                for i in range(PAIR):
-                    empty_bank(banks[pair * PAIR + i], stage, i, vector_helps and i % 2 == 1)
-                result.append(stage)
-            return result
-
-        def project(rows, weight_name, half, tag):
+        def project(rows, weight_name, half):
             codes, scales = operand[rows]
             w_codes, w_scales = weight_mx[(weight_name, half)]
-            bank = psum.tile([P, BANK], F32, tag=tag)
+            bank = psum.tile([P, BANK], F32, tag="kp")
             for g in range(PASSES):
                 nc.tensor.matmul_mx(
                     out=bank,
@@ -142,137 +142,144 @@ def tile_multiheadattention_pa_kernel(tc, query, keys, Wq, Wk, out):
                     start=(g == 0),
                     stop=(g == PASSES - 1),
                 )
-            return bank.rearrange("p (h j) -> p h j", j=HEAD_DIM)
+            return bank
 
         query_stage = stages.tile([P, PASSES, 1, P, PACK], BF16, align_bytes=64, tag="query_stage", bufs=1)
         empty_bank(transpose_tile("q", 0, "xt"), query_stage, 0, False)
-        qp = keep.tile([P, HALVES, BANK_HEADS, HEAD_DIM], F32)
-
-        def project_query():
-            for half in range(HALVES):
-                bank = project(("q", 0), "wq", half, "kp")
-                nc.scalar.activation(out=qp[:, half], in_=bank, func=ACT.Copy, scale=HEAD_DIM**-0.5)
-
         previous = None
         for name in ("wq", "wk"):
             for first in range(0, CHAN // P, PAIR):
-                stage = transpose_run(name, first, PAIR, ("kp", "xt"), first % QUAD == 0)[0]
+                stage = transpose_pair(name, first, ("kp", "xt"), first % (2 * PAIR) == 0)
                 if previous is None:
                     quantise_rows(query_stage, "q", 0, keep)
                 else:
                     quantise_weight_pair(*previous)
                 previous = (stage, name, first)
-                if (name, first) == ("wk", 99):
-                    project_query()
+
+        key_stage = {}
+
+        def transpose_keys(n):
+            if n < PAIRS:
+                key_stage[n] = transpose_pair("k", n * PAIR, ("xt", "xt"), False)
+
+        transpose_keys(0)
+        quantise_weight_pair(*previous)
+        quantise_rows(key_stage[0], "k", 0, packed)
+
+        qp = keep.tile([P, HALVES, BANK], F32)
+        for half in range(HALVES):
+            bank = project(("q", 0), "wq", half)
+            nc.scalar.activation(out=qp[:, half], in_=bank, func=ACT.Copy, scale=HEAD_DIM**-0.5)
 
         dot = keep.tile([P, HEADS, SEQ], F32)
 
-        def multiply(tiles, by_half):
-            result = {}
+        def multiply(tiles, order):
+            products = []
             for s in tiles:
-                product = prods.tile([P, HALVES, BANK_HEADS, HEAD_DIM], F32)
-                result[s] = product
-            order = [(s, half) for s in tiles for half in range(HALVES)]
-            if by_half:
-                order = [(s, half) for half in range(HALVES) for s in tiles]
-            for s, half in order:
-                kp = project(("k", s), "wk", half, "kp")
-                nc.vector.tensor_tensor(out=result[s][:, half], in0=kp, in1=qp[:, half], op=ALU.mult)
-            return {s: product.rearrange("p n h j -> p (n h) j") for s, product in result.items()}
+                product = prods.tile([P, HALVES, BANK], F32)
+                products.append(product)
+            for i, half in order:
+                kp = project(("k", tiles[i]), "wk", half)
+                nc.vector.tensor_tensor(out=products[i][:, half], in0=kp, in1=qp[:, half], op=ALU.mult)
+            return products
 
-        def sum_on_scalar(product, s):
-            unread = scrap.tile([P, HEADS, HEAD_DIM], F32)
-            for h in range(HEADS):
-                nc.scalar.activation(
-                    out=unread[:, h, :], in_=product[:, h, :], func=ACT.Copy, accum_out=dot[:, h, s : s + 1]
-                )
+        def head_runs(product, half, h):
+            runs = product[:, half].rearrange("p (v i h r) -> p v i h r", v=BANK_PAIRS, i=PAIR, h=GROUP_HEADS)
+            return runs[:, h // GROUP_HEADS, :, h % GROUP_HEADS, :]
 
-        def sum_on_vector(product, s):
-            nc.vector.tensor_reduce(out=dot[:, :, s], in_=product, axis=AXIS_X, op=ALU.add)
+        def sum_on_scalar(product, s, halves):
+            for half in halves:
+                unread = scrap.tile([P, HALF_HEADS, PAIR, PART], F32)
+                for h in range(HALF_HEADS):
+                    column = half * HALF_HEADS + h
+                    nc.scalar.activation(
+                        out=unread[:, h],
+                        in_=head_runs(product, half, h),
+                        func=ACT.Copy,
+                        accum_out=dot[:, column, s : s + 1],
+                    )
+
+        def sum_on_vector(product, s, halves):
+            for half in halves:
+                runs = product[:, half].rearrange("p (v i h r) -> p v h i r", v=BANK_PAIRS, i=PAIR, h=GROUP_HEADS)
+                for v in range(BANK_PAIRS):
+                    column = half * HALF_HEADS + v * GROUP_HEADS
+                    nc.vector.tensor_reduce(
+                        out=dot[:, column : column + GROUP_HEADS, s], in_=runs[:, v], axis=AXIS_XY, op=ALU.add
+                    )
 
         half_folded = []
+        folded = []
 
-        def fold(source, width):
-            folded = folds.tile([P, HEADS, width], F32, tag="folded%d" % width, bufs=4 if width == FOLD_WIDTHS[-1] else 2)
-            nc.gpsimd.tensor_tensor(
-                out=folded, in0=source[:, :, 0:width], in1=source[:, :, width : 2 * width], op=ALU.add
-            )
-            return folded
+        def fold(shape, left, right, tag, bufs):
+            result = folds.tile(shape, F32, tag=tag, bufs=bufs)
+            nc.gpsimd.tensor_tensor(out=result, in0=left, in1=right, op=ALU.add)
+            return result
 
         def last_fold():
             source, s = half_folded.pop()
-            folded_tiles.append((fold(source, FOLD_WIDTHS[2]), s))
+            quarter = PART // 4
+            if not folded or len(folded[-1][1]) == 2:
+                result = folds.tile([P, 2, HEADS, quarter], F32, tag="folded8", bufs=3)
+                folded.append((result, []))
+            result, tiles = folded[-1]
+            nc.gpsimd.tensor_tensor(out=result[:, len(tiles)], in0=source[:, :, 0:quarter], in1=source[:, :, quarter : 2 * quarter], op=ALU.add)
+            tiles.append(s)
 
         def fold_on_gpsimd(product, s):
-            folded = fold(product, FOLD_WIDTHS[0])
+            runs = product.rearrange("p n (v i c) -> p (n v) i c", v=BANK_PAIRS, i=PAIR)
+            once = fold([P, HALVES * BANK_PAIRS, P], runs[:, :, 0, :], runs[:, :, 1, :], "folded32", 2)
             if half_folded:
                 last_fold()
-            half_folded.append((fold(folded, FOLD_WIDTHS[1]), s))
+            heads = once.rearrange("p v (h r) -> p (v h) r", r=PART)
+            middle = PART // 2
+            twice = fold([P, HEADS, middle], heads[:, :, 0:middle], heads[:, :, middle:PART], "folded16", 2)
+            half_folded.append((twice, s))
 
-        chunks = [(s, 2) for s in range(0, SEQ, 2)]
-        summers = "SG" * 15 + "SV"
-        to_sum = []
-        folded_tiles = []
-        staged = {}
+        def sum_folded():
+            source, tiles = folded.pop(0)
+            if len(tiles) == 2:
+                nc.vector.tensor_reduce(
+                    out=dot[:, :, tiles[0] : tiles[1] + 1 : PAIR].rearrange("p h s -> p s h"), in_=source, axis=AXIS_X, op=ALU.add
+                )
+            else:
+                nc.vector.tensor_reduce(out=dot[:, :, tiles[0]], in_=source[:, 0], axis=AXIS_X, op=ALU.add)
 
-        def transpose_chunk(n):
-            if n < len(chunks):
-                first, count = chunks[n]
-                new_stages = transpose_run("k", first, count, ("xt",), False)
-                for pair, stage in enumerate(new_stages):
-                    staged[first + pair * PAIR] = stage
-
-        transpose_chunk(0)
-        quantise_weight_pair(*previous)
-        quantise_rows(staged[0], "k", 0, packed)
-        transpose_chunk(1)
-        project_query()
-        for n in range(len(chunks)):
+        both = tuple(range(HALVES))
+        by_tile = ((0, 0), (0, 1))
+        for n in range(PAIRS - 1):
+            transpose_keys(n + 1)
+            (first_product,) = multiply([n * PAIR], by_tile)
+            fold_on_gpsimd(first_product, n * PAIR)
+            if len(folded) > 1:
+                sum_folded()
+            quantise_rows(key_stage[n + 1], "k", (n + 1) * PAIR, packed)
+            (second_product,) = multiply([n * PAIR + 1], by_tile)
             if n > 0:
-                transpose_chunk(n + 2 - 0)
-            waiting = []
-            if n + 1 < len(chunks):
-                waiting = [chunks[n + 1][0] + i for i in range(0, chunks[n + 1][1], PAIR)]
-            fresh = []
-            for i in range(chunks[n][1]):
-                s = chunks[n][0] + i
-                if n > 0 and i % PAIR == 0 and waiting:
-                    quantise_rows(staged[waiting[0]], "k", waiting.pop(0), packed)
-                if n == 0 and i == 0:
-                    product_of = multiply(list(range(chunks[0][1])), False)
-                elif n > 0:
-                    product_of = multiply([s], False)
-                product = product_of[s]
-                if summers[s] == "G":
-                    fold_on_gpsimd(product, s)
-                    if s == 29:
-                        last_fold()
-                elif summers[s] == "V":
-                    sum_on_vector(product, s)
-                else:
-                    fresh.append((product, s))
-                if i % 2 == 0 and len(folded_tiles) > 1:
-                    sum_on_vector(*folded_tiles.pop(0))
-            while waiting:
-                quantise_rows(staged[waiting[0]], "k", waiting.pop(0), packed)
-            if n == 0:
-                transpose_chunk(2)
-            for product, s in fresh:
-                sum_on_scalar(product, s)
-        while folded_tiles:
-            sum_on_vector(*folded_tiles.pop(0))
+                sum_on_scalar(*to_sum)
+            to_sum = (second_product, n * PAIR + 1, both)
+        last_fold()
+        last = SEQ - PAIR
+        products = multiply([last, last + 1], ((0, 0), (1, 0), (0, 1), (1, 1)))
+        sum_on_scalar(*to_sum)
+        sum_on_scalar(products[0], last, (0,))
+        sum_on_scalar(products[1], last + 1, (0,))
+        while folded:
+            sum_folded()
+        sum_on_vector(products[0], last, (1,))
+        sum_on_vector(products[1], last + 1, (1,))
 
         top = keep.tile([P, HEADS], F32)
         shifted = keep.tile([P, HEADS, SEQ], F32)
         grown = keep.tile([P, HEADS, SEQ], F32)
         total = keep.tile([P, HEADS], F32)
         for half in range(HALVES):
-            heads = slice(half * BANK_HEADS, (half + 1) * BANK_HEADS)
+            heads = slice(half * HALF_HEADS, (half + 1) * HALF_HEADS)
             nc.vector.tensor_reduce(out=top[:, heads], in_=dot[:, heads], axis=AXIS_X, op=ALU.max)
             nc.vector.tensor_tensor(
                 out=shifted[:, heads],
                 in0=dot[:, heads],
-                in1=top[:, heads].unsqueeze(2).to_broadcast([P, BANK_HEADS, SEQ]),
+                in1=top[:, heads].unsqueeze(2).to_broadcast([P, HALF_HEADS, SEQ]),
                 op=ALU.subtract,
             )
             nc.scalar.activation(out=grown[:, heads], in_=shifted[:, heads], func=ACT.Exp)

@@ -23,6 +23,7 @@ CHAN = HEADS * HEAD_DIM
 PASSES = FEAT // (P * PACK)
 PAIR = 2
 PAIRS = SEQ // PAIR
+QUAD = 4
 GROUP = PAIR * P
 HALVES = 2
 BANK = CHAN // HALVES
@@ -40,7 +41,8 @@ def tile_multiheadattention_pa_kernel(tc, query, keys, Wq, Wk, out):
         ctx.enter_context(tc.manual_schedule())
         raw = ctx.enter_context(tc.tile_pool(name="raw", bufs=1))
         keep = ctx.enter_context(tc.tile_pool(name="keep", bufs=1))
-        stages = ctx.enter_context(tc.tile_pool(name="stages", bufs=6))
+        stages = ctx.enter_context(tc.tile_pool(name="stages", bufs=3))
+        singles = ctx.enter_context(tc.tile_pool(name="singles", bufs=2))
         packed = ctx.enter_context(tc.tile_pool(name="packed", bufs=3))
         prods = ctx.enter_context(tc.tile_pool(name="prods", bufs=7))
         folds = ctx.enter_context(tc.tile_pool(name="folds", bufs=2))
@@ -88,12 +90,10 @@ def tile_multiheadattention_pa_kernel(tc, query, keys, Wq, Wk, out):
             else:
                 nc.scalar.copy(out=target, in_=bank.rearrange("p g u r -> p g r u"))
 
-        def transpose_pair(name, first, tags, vector_helps):
+        def transpose_pair(name, first, tags, stage, place, vector_helps):
             banks = [transpose_tile(name, first + i, tags[i]) for i in range(PAIR)]
-            stage = stages.tile([P, PASSES, PAIR, P, PACK], BF16, align_bytes=64)
             for i in range(PAIR):
-                empty_bank(banks[i], stage, i, vector_helps and i == 1)
-            return stage
+                empty_bank(banks[i], stage, place + i, vector_helps and i == 1)
 
         def quantise(stage_part, codes_part, scales_part):
             nc.vector.quantize_mx(out=codes_part.bitcast(FP8X4), scales=scales_part, in_=stage_part)
@@ -121,12 +121,12 @@ def tile_multiheadattention_pa_kernel(tc, query, keys, Wq, Wk, out):
                     keep.tile([P, PASSES, BANK], U8, align_bytes=64, name="%s_scales%d" % (name, half)),
                 )
 
-        def quantise_weight_pair(stage, name, first):
-            half, place = divmod(first // PAIR, BANK_PAIRS)
+        def quantise_weights(stage, name, half, first, count):
             codes, scales = weight_mx[(name, half)]
-            cols = slice(place * GROUP, (place + 1) * GROUP)
+            cols = slice(first * P, (first + count) * P)
             for g in range(PASSES):
-                quantise(stage[:, g].rearrange("p i r t -> p (i r t)"), codes[:, g, cols], scales[:, g, cols])
+                part = stage[:, g, first : first + count]
+                quantise(part.rearrange("p i r t -> p (i r t)"), codes[:, g, cols], scales[:, g, cols])
 
         def project(rows, weight_name, half):
             codes, scales = operand[rows]
@@ -146,30 +146,49 @@ def tile_multiheadattention_pa_kernel(tc, query, keys, Wq, Wk, out):
 
         query_stage = stages.tile([P, PASSES, 1, P, PACK], BF16, align_bytes=64, tag="query_stage", bufs=1)
         empty_bank(transpose_tile("q", 0, "xt"), query_stage, 0, False)
-        previous = None
+        qp = keep.tile([P, HALVES, BANK], F32)
+
+        def project_query(half):
+            bank = project(("q", 0), "wq", half)
+            nc.scalar.activation(out=qp[:, half], in_=bank, func=ACT.Copy, scale=HEAD_DIM**-0.5)
+
+        waiting = [(query_stage,)]
         for name in ("wq", "wk"):
-            for first in range(0, CHAN // P, PAIR):
-                stage = transpose_pair(name, first, ("kp", "xt"), first % (2 * PAIR) == 0)
-                if previous is None:
-                    quantise_rows(query_stage, "q", 0, keep)
-                else:
-                    quantise_weight_pair(*previous)
-                previous = (stage, name, first)
+            for half in range(HALVES):
+                stage = stages.tile([P, PASSES, QUAD, P, PACK], BF16, align_bytes=64, tag="weight_stage", bufs=2)
+                for place in range(0, QUAD, PAIR):
+                    transpose_pair(name, half * QUAD + place, ("kp", "xt"), stage, place, place == PAIR)
+                    if waiting:
+                        part = waiting.pop(0)
+                        if len(part) == 1:
+                            quantise_rows(part[0], "q", 0, keep)
+                        else:
+                            quantise_weights(*part)
+                    if (name, half) == ("wk", 1):
+                        waiting.append((stage, name, half, place, PAIR))
+                    elif place + PAIR == QUAD:
+                        waiting.append((stage, name, half, 0, QUAD))
+                    if (name, half, place) == ("wk", 0, 0):
+                        project_query(0)
+                    if (name, half, place) == ("wk", 0, 2):
+                        project_query(1)
 
         key_stage = {}
 
         def transpose_keys(n):
             if n < PAIRS:
-                key_stage[n] = transpose_pair("k", n * PAIR, ("xt", "xt"), False)
+                stage = stages.tile([P, PASSES, PAIR, P, PACK], BF16, align_bytes=64, tag="key_stage")
+                transpose_pair("k", n * PAIR, ("xt", "xt"), stage, 0, False)
+                key_stage[n] = stage
 
-        transpose_keys(0)
-        quantise_weight_pair(*previous)
-        quantise_rows(key_stage[0], "k", 0, packed)
-
-        qp = keep.tile([P, HALVES, BANK], F32)
-        for half in range(HALVES):
-            bank = project(("q", 0), "wq", half)
-            nc.scalar.activation(out=qp[:, half], in_=bank, func=ACT.Copy, scale=HEAD_DIM**-0.5)
+        first_stages = []
+        for i in range(PAIR):
+            stage = stages.tile([P, PASSES, 1, P, PACK], BF16, align_bytes=64, tag="single_stage", bufs=PAIR)
+            empty_bank(transpose_tile("k", i, "xt"), stage, 0, False)
+            first_stages.append(stage)
+        quantise_rows(first_stages[0], "k", 0, singles)
+        quantise_weights(*waiting.pop(0))
+        quantise_rows(first_stages[1], "k", 1, singles)
 
         dot = keep.tile([P, HEADS, SEQ], F32)
 

@@ -170,8 +170,6 @@ def tile_multiheadattention_pa_kernel(tc, query, keys, Wq, Wk, out):
                         waiting.append((stage, name, half, 0, QUAD))
                     if (name, half, place) == ("wk", 0, 0):
                         project_query(0)
-                    if (name, half, place) == ("wk", 0, 2):
-                        project_query(1)
 
         key_stage = {}
 
@@ -268,6 +266,8 @@ def tile_multiheadattention_pa_kernel(tc, query, keys, Wq, Wk, out):
         by_tile = ((0, 0), (0, 1))
         for n in range(PAIRS - 1):
             transpose_keys(n + 1)
+            if n == 0:
+                project_query(1)
             (first_product,) = multiply([n * PAIR], by_tile)
             fold_on_gpsimd(first_product, n * PAIR)
             if len(folded) > 1:

from contextlib import ExitStack

import concourse.mybir as mybir
from concourse.masks import make_identity

F32 = mybir.dt.float32
BF16 = mybir.dt.bfloat16
U32 = mybir.dt.uint32
U8 = mybir.dt.uint8
FP8X4 = mybir.dt.float8_e4m3fn_x4
ALU = mybir.AluOpType
ACT = mybir.ActivationFunctionType
AXIS_X = mybir.AxisListType.X
AXIS_XY = mybir.AxisListType.XY

P = 128
PACK = 4
SEQ = 32
FEAT = 1024
HEADS = 16
HEAD_DIM = 64
CHAN = HEADS * HEAD_DIM
PASSES = FEAT // (P * PACK)
PAIR = 2
PAIRS = SEQ // PAIR
QUAD = 4
GROUP = PAIR * P
HALVES = 2
BANK = CHAN // HALVES
BANK_PAIRS = BANK // GROUP
GROUP_HEADS = GROUP // HEAD_DIM
HALF_HEADS = HEADS // HALVES
PART = HEAD_DIM // PAIR

FLOPS = 2 * (SEQ + 1) * P * FEAT * CHAN


def tile_multiheadattention_pa_kernel(tc, query, keys, Wq, Wk, out):
    nc = tc.nc
    with ExitStack() as ctx:
        ctx.enter_context(tc.manual_schedule())
        raw = ctx.enter_context(tc.tile_pool(name="raw", bufs=1))
        keep = ctx.enter_context(tc.tile_pool(name="keep", bufs=1))
        stages = ctx.enter_context(tc.tile_pool(name="stages", bufs=3))
        singles = ctx.enter_context(tc.tile_pool(name="singles", bufs=2))
        packed = ctx.enter_context(tc.tile_pool(name="packed", bufs=3))
        prods = ctx.enter_context(tc.tile_pool(name="prods", bufs=7))
        folds = ctx.enter_context(tc.tile_pool(name="folds", bufs=2))
        scrap = ctx.enter_context(tc.tile_pool(name="scrap", bufs=2))
        psum = ctx.enter_context(tc.psum_pool(name="psum", bufs=4))

        raw_tiles = {}

        def load_pair(name, first, source):
            rows = raw.tile([P, PAIR, FEAT], BF16, name="%s_raw%d" % (name, first))
            nc.sync.dma_start(out=rows, in_=source)
            for i in range(PAIR):
                raw_tiles[(name, first + i)] = rows[:, i, :]

        query_raw = raw.tile([P, FEAT], BF16)
        nc.sync.dma_start(out=query_raw, in_=query)
        raw_tiles[("q", 0)] = query_raw
        for name, weight in (("wq", Wq), ("wk", Wk)):
            for first in range(0, CHAN // P, PAIR):
                source = weight[first * P : (first + PAIR) * P, :]
                load_pair(name, first, source.rearrange("(p i) k -> p i k", i=PAIR))
        for s in range(0, SEQ, PAIR):
            load_pair("k", s, keys[s : s + PAIR].rearrange("s b k -> b s k"))

        ident = keep.tile([P, P], F32)
        make_identity(nc, ident)

        warm = keep.tile([P, 1], F32)
        nc.vector.memset(warm, 0.0)
        nc.scalar.activation(out=warm, in_=warm, func=ACT.Exp)

        def transpose_tile(name, i, tag):
            words = raw_tiles[(name, i)].bitcast(F32)
            bank = psum.tile([P, PASSES, 2, P], F32, tag=tag)
            for g in range(PASSES):
                for u in range(2):
                    every_second = words[:, 2 * g * P + u : 2 * (g + 1) * P : 2]
                    nc.tensor.transpose(bank[:, g, u, :], every_second, ident)
            return bank

        def empty_bank(bank, stage, i, on_vector):
            target = stage.bitcast(F32)[:, :, i, :, :]
            if on_vector:
                nc.vector.tensor_copy(out=target, in_=bank.rearrange("p g u r -> p g r u"))
            else:
                nc.scalar.copy(out=target, in_=bank.rearrange("p g u r -> p g r u"))

        def transpose_pair(name, first, tags, stage, place, vector_helps):
            banks = [transpose_tile(name, first + i, tags[i]) for i in range(PAIR)]
            for i in range(PAIR):
                empty_bank(banks[i], stage, place + i, vector_helps and i == 1)

        def quantise(stage_part, codes_part, scales_part):
            nc.vector.quantize_mx(out=codes_part.bitcast(FP8X4), scales=scales_part, in_=stage_part)

        operand = {}

        def quantise_rows(stage, name, first, pool):
            count = stage.shape[2]
            codes = pool.tile([P, PASSES, count * P], U32, align_bytes=64, name="%s_codes" % name)
            scales = pool.tile([P, PASSES, count * P], U8, align_bytes=64, name="%s_scales" % name)
            quantise(
                stage.rearrange("p g i r t -> p (g i r t)"),
                codes.rearrange("p g c -> p (g c)"),
                scales.rearrange("p g c -> p (g c)"),
            )
            for i in range(count):
                cols = slice(i * P, (i + 1) * P)
                operand[(name, first + i)] = (codes[:, :, cols], scales[:, :, cols])

        weight_mx = {}
        for name in ("wq", "wk"):
            for half in range(HALVES):
                weight_mx[(name, half)] = (
                    keep.tile([P, PASSES, BANK], U32, align_bytes=64, name="%s_codes%d" % (name, half)),
                    keep.tile([P, PASSES, BANK], U8, align_bytes=64, name="%s_scales%d" % (name, half)),
                )

        def quantise_weights(stage, name, half, first, count):
            codes, scales = weight_mx[(name, half)]
            cols = slice(first * P, (first + count) * P)
            for g in range(PASSES):
                part = stage[:, g, first : first + count]
                quantise(part.rearrange("p i r t -> p (i r t)"), codes[:, g, cols], scales[:, g, cols])

        def project(rows, weight_name, half):
            codes, scales = operand[rows]
            w_codes, w_scales = weight_mx[(weight_name, half)]
            bank = psum.tile([P, BANK], F32, tag="kp")
            for g in range(PASSES):
                nc.tensor.matmul_mx(
                    out=bank,
                    lhsT=codes[:, g, :].bitcast(FP8X4),
                    lhsT_scale=scales[:, g, :],
                    rhs=w_codes[:, g, :].bitcast(FP8X4),
                    rhs_scale=w_scales[:, g, :],
                    start=(g == 0),
                    stop=(g == PASSES - 1),
                )
            return bank

        query_stage = stages.tile([P, PASSES, 1, P, PACK], BF16, align_bytes=64, tag="query_stage", bufs=1)
        empty_bank(transpose_tile("q", 0, "xt"), query_stage, 0, False)
        qp = keep.tile([P, HALVES, BANK], F32)

        def project_query(half):
            bank = project(("q", 0), "wq", half)
            nc.scalar.activation(out=qp[:, half], in_=bank, func=ACT.Copy, scale=HEAD_DIM**-0.5)

        waiting = [(query_stage,)]
        for name in ("wq", "wk"):
            for half in range(HALVES):
                stage = stages.tile([P, PASSES, QUAD, P, PACK], BF16, align_bytes=64, tag="weight_stage", bufs=2)
                for place in range(0, QUAD, PAIR):
                    transpose_pair(name, half * QUAD + place, ("kp", "xt"), stage, place, place == PAIR)
                    if waiting:
                        part = waiting.pop(0)
                        if len(part) == 1:
                            quantise_rows(part[0], "q", 0, keep)
                        else:
                            quantise_weights(*part)
                    if (name, half) == ("wk", 1):
                        waiting.append((stage, name, half, place, PAIR))
                    elif place + PAIR == QUAD:
                        waiting.append((stage, name, half, 0, QUAD))
                    if (name, half, place) == ("wk", 0, 0):
                        project_query(0)

        key_stage = {}

        def transpose_keys(n):
            if n < PAIRS:
                stage = stages.tile([P, PASSES, PAIR, P, PACK], BF16, align_bytes=64, tag="key_stage")
                transpose_pair("k", n * PAIR, ("xt", "xt"), stage, 0, False)
                key_stage[n] = stage

        first_stages = []
        for i in range(PAIR):
            stage = stages.tile([P, PASSES, 1, P, PACK], BF16, align_bytes=64, tag="single_stage", bufs=PAIR)
            empty_bank(transpose_tile("k", i, "xt"), stage, 0, False)
            first_stages.append(stage)
        quantise_rows(first_stages[0], "k", 0, singles)
        quantise_weights(*waiting.pop(0))
        quantise_rows(first_stages[1], "k", 1, singles)

        dot = keep.tile([P, HEADS, SEQ], F32)

        def multiply(tiles, order):
            products = []
            for s in tiles:
                product = prods.tile([P, HALVES, BANK], F32)
                products.append(product)
            for i, half in order:
                kp = project(("k", tiles[i]), "wk", half)
                nc.vector.tensor_tensor(out=products[i][:, half], in0=kp, in1=qp[:, half], op=ALU.mult)
            return products

        def head_runs(product, half, h):
            runs = product[:, half].rearrange("p (v i h r) -> p v i h r", v=BANK_PAIRS, i=PAIR, h=GROUP_HEADS)
            return runs[:, h // GROUP_HEADS, :, h % GROUP_HEADS, :]

        def sum_on_scalar(product, s, halves):
            for half in halves:
                unread = scrap.tile([P, HALF_HEADS, PAIR, PART], F32)
                for h in range(HALF_HEADS):
                    column = half * HALF_HEADS + h
                    nc.scalar.activation(
                        out=unread[:, h],
                        in_=head_runs(product, half, h),
                        func=ACT.Copy,
                        accum_out=dot[:, column, s : s + 1],
                    )

        def sum_on_vector(product, s, halves):
            for half in halves:
                runs = product[:, half].rearrange("p (v i h r) -> p v h i r", v=BANK_PAIRS, i=PAIR, h=GROUP_HEADS)
                for v in range(BANK_PAIRS):
                    column = half * HALF_HEADS + v * GROUP_HEADS
                    nc.vector.tensor_reduce(
                        out=dot[:, column : column + GROUP_HEADS, s], in_=runs[:, v], axis=AXIS_XY, op=ALU.add
                    )

        half_folded = []
        folded = []

        def fold(shape, left, right, tag, bufs):
            result = folds.tile(shape, F32, tag=tag, bufs=bufs)
            nc.gpsimd.tensor_tensor(out=result, in0=left, in1=right, op=ALU.add)
            return result

        def last_fold():
            source, s = half_folded.pop()
            quarter = PART // 4
            if not folded or len(folded[-1][1]) == 2:
                result = folds.tile([P, 2, HEADS, quarter], F32, tag="folded8", bufs=3)
                folded.append((result, []))
            result, tiles = folded[-1]
            nc.gpsimd.tensor_tensor(out=result[:, len(tiles)], in0=source[:, :, 0:quarter], in1=source[:, :, quarter : 2 * quarter], op=ALU.add)
            tiles.append(s)

        def fold_on_gpsimd(product, s):
            runs = product.rearrange("p n (v i c) -> p (n v) i c", v=BANK_PAIRS, i=PAIR)
            once = fold([P, HALVES * BANK_PAIRS, P], runs[:, :, 0, :], runs[:, :, 1, :], "folded32", 2)
            if half_folded:
                last_fold()
            heads = once.rearrange("p v (h r) -> p (v h) r", r=PART)
            middle = PART // 2
            twice = fold([P, HEADS, middle], heads[:, :, 0:middle], heads[:, :, middle:PART], "folded16", 2)
            half_folded.append((twice, s))

        def sum_folded():
            source, tiles = folded.pop(0)
            if len(tiles) == 2:
                nc.vector.tensor_reduce(
                    out=dot[:, :, tiles[0] : tiles[1] + 1 : PAIR].rearrange("p h s -> p s h"), in_=source, axis=AXIS_X, op=ALU.add
                )
            else:
                nc.vector.tensor_reduce(out=dot[:, :, tiles[0]], in_=source[:, 0], axis=AXIS_X, op=ALU.add)

        both = tuple(range(HALVES))
        by_tile = ((0, 0), (0, 1))
        for n in range(PAIRS - 1):
            transpose_keys(n + 1)
            if n == 0:
                project_query(1)
            (first_product,) = multiply([n * PAIR], by_tile)
            fold_on_gpsimd(first_product, n * PAIR)
            if len(folded) > 1:
                sum_folded()
            quantise_rows(key_stage[n + 1], "k", (n + 1) * PAIR, packed)
            (second_product,) = multiply([n * PAIR + 1], by_tile)
            if n > 0:
                sum_on_scalar(*to_sum)
            to_sum = (second_product, n * PAIR + 1, both)
        last_fold()
        last = SEQ - PAIR
        products = multiply([last, last + 1], ((0, 0), (1, 0), (0, 1), (1, 1)))
        sum_on_scalar(*to_sum)
        sum_on_scalar(products[0], last, (0,))
        sum_on_scalar(products[1], last + 1, (0,))
        while folded:
            sum_folded()
        sum_on_vector(products[0], last, (1,))
        sum_on_vector(products[1], last + 1, (1,))

        top = keep.tile([P, HEADS], F32)
        shifted = keep.tile([P, HEADS, SEQ], F32)
        grown = keep.tile([P, HEADS, SEQ], F32)
        total = keep.tile([P, HEADS], F32)
        for half in range(HALVES):
            heads = slice(half * HALF_HEADS, (half + 1) * HALF_HEADS)
            nc.vector.tensor_reduce(out=top[:, heads], in_=dot[:, heads], axis=AXIS_X, op=ALU.max)
            nc.vector.tensor_tensor(
                out=shifted[:, heads],
                in0=dot[:, heads],
                in1=top[:, heads].unsqueeze(2).to_broadcast([P, HALF_HEADS, SEQ]),
                op=ALU.subtract,
            )
            nc.scalar.activation(out=grown[:, heads], in_=shifted[:, heads], func=ACT.Exp)
        nc.scalar.activation(out=warm, in_=warm, func=ACT.Ln)
        nc.vector.tensor_reduce(out=total, in_=grown, axis=AXIS_X, op=ALU.add)
        log_total = keep.tile([P, HEADS], F32)
        nc.scalar.activation(out=log_total, in_=total, func=ACT.Ln)
        result = keep.tile([P, SEQ, HEADS], F32)
        part = SEQ // 2
        for first, queue in ((0, nc.sync), (part, nc.scalar)):
            nc.vector.tensor_tensor(
                out=result[:, first : first + part, :],
                in0=shifted[:, :, first : first + part].rearrange("p h s -> p s h"),
                in1=log_total.unsqueeze(1).to_broadcast([P, part, HEADS]),
                op=ALU.subtract,
            )
            queue.dma_start(
                out=out[first : first + part].rearrange("s b h -> b s h"),
                in_=result[:, first : first + part, :],
            )
